import numpy as np
import ml_dtypes

BF16 = ml_dtypes.bfloat16


def bf(x):
    return np.asarray(x, np.float32).astype(BF16)


def f32(x):
    return np.asarray(x, np.float32)


def f64(x):
    return np.asarray(x).astype(np.float64)


def striped(idx):
    return np.tile(idx.reshape(-1, 16).T, (8, 1))


F, K, C, S, N = 2, 128, 128, 256, 128
DENS = 0.0625


def sigmoid(v):
    return 1.0 / (1.0 + np.exp(-v))


def setup_inputs():
    a = np.random.uniform(size=(F, N, N)) * (np.random.uniform(size=(F, N, N)) < DENS)
    a[:, np.arange(N), np.arange(N)] = 1.0
    return {"base": f32(0.5 * np.random.standard_normal((C, S))), "x": bf(np.random.standard_normal((K, N))), "w": bf(np.random.standard_normal((K, C)) / np.sqrt(K)), "adjT": bf(a), "b": f32(0.3 * np.random.standard_normal((C, 1))), "offs": striped(np.random.permutation(S)[:N])}


def reference(base, x, w, adjT, b, offs):
    idx = offs[:16].T.reshape(-1)
    a = f64(adjT)
    d = 1.0 / np.sqrt(a.sum(axis=1))
    an = (d[:, :, None] * a * d[:, None, :]).sum(axis=0)
    h = f64(x).T @ f64(w)
    v = h.T @ an + f64(b)
    out = f64(base).copy()
    out[:, idx] = v * sigmoid(v)
    return out

@@ -1,0 +1,74 @@
+import concourse.mybir as mybir
+
+F32 = mybir.dt.float32
+BF16 = mybir.dt.bfloat16
+U16 = mybir.dt.uint16
+ACT = mybir.ActivationFunctionType
+ALU = mybir.AluOpType
+
+P = 128
+E = 2
+SLOTS = 256
+
+FLOPS = 2 * P * P * P * 2
+
+
+def tile_densegcn_kernel(tc, base, x, w, adjT, b, offs, out):
+    nc = tc.nc
+    with tc.tile_pool(name="held", bufs=1) as held, tc.psum_pool(name="psum", bufs=1) as psum:
+        adj = held.tile([P, E * P], BF16, name="adj")
+        nc.sync.dma_start(adj[:, 0:P], adjT[0])
+        nc.scalar.dma_start(adj[:, P : 2 * P], adjT[1])
+        offsets = held.tile([P, P // 16], U16, name="offsets")
+        nc.sync.dma_start(offsets[:], offs)
+        x_sb = held.tile([P, P], BF16, name="x_sb")
+        nc.sync.dma_start(x_sb[:], x)
+        w_sb = held.tile([P, P], BF16, name="w_sb")
+        nc.scalar.dma_start(w_sb[:], w)
+        window = held.tile([P, SLOTS], F32, name="window")
+        nc.gpsimd.dma_start(window[:], base)
+        bias = held.tile([P, 1], F32, name="bias")
+        nc.gpsimd.dma_start(bias[:], b)
+
+        ones = held.tile([P, P], BF16, name="ones")
+        nc.vector.memset(ones[:], 1.0)
+
+        deg = psum.tile([P, E * P + E], F32, name="deg")
+        nc.tensor.matmul(deg[:, 0 : E * P], ones[:], adj[:], start=True, stop=True)
+        for e in range(E):
+            nc.tensor.matmul(
+                deg[:, E * P + e : E * P + e + 1], adj[:, e * P : (e + 1) * P], ones[:, 0:1], start=True, stop=True
+            )
+        root = held.tile([P, E * P + E], F32, name="root")
+        nc.scalar.activation(root[:], deg[:], ACT.Sqrt)
+        d = held.tile([P, E * P + E], F32, name="d")
+        nc.vector.reciprocal(d[:], root[:])
+
+        part0 = held.tile([P, P], F32, name="part0")
+        part1 = held.tile([P, P], F32, name="part1")
+        for e, part in enumerate((part0, part1)):
+            nc.vector.scalar_tensor_tensor(
+                part[:],
+                adj[:, e * P : (e + 1) * P],
+                d[:, E * P + e : E * P + e + 1],
+                d[:, e * P : (e + 1) * P],
+                ALU.mult,
+                ALU.mult,
+            )
+        an = held.tile([P, P], BF16, name="an")
+        nc.vector.tensor_tensor(an[:], part0[:], part1[:], ALU.add)
+
+        h_ps = psum.tile([P, P], F32, name="h_ps")
+        nc.tensor.matmul(h_ps[:], x_sb[:], w_sb[:], start=True, stop=True)
+        h = held.tile([P, P], BF16, name="h")
+        nc.vector.tensor_copy(h[:], h_ps[:])
+
+        v_ps = psum.tile([P, P], F32, name="v_ps")
+        nc.tensor.matmul(v_ps[:], h[:], an[:], start=True, stop=True)
+        sig = held.tile([P, P], F32, name="sig")
+        nc.scalar.activation(sig[:], v_ps[:], ACT.Sigmoid, bias=bias[:])
+        v = held.tile([P, P], F32, name="v")
+        nc.vector.tensor_scalar(v[:], v_ps[:], bias[:], None, ALU.add)
+
+        nc.vector.tensor_tensor(window[:].indirect(offsets[:]), v[:], sig[:], ALU.mult)
+        nc.sync.dma_start(out, window[:])

@@ -39,10 +39,8 @@ def tile_densegcn_kernel(tc, base, x, w, adjT, b, offs, out):
             nc.tensor.matmul(
                 deg[:, E * P + e : E * P + e + 1], adj[:, e * P : (e + 1) * P], ones[:, 0:1], start=True, stop=True
             )
-        root = held.tile([P, E * P + E], F32, name="root")
-        nc.scalar.activation(root[:], deg[:], ACT.Sqrt)
         d = held.tile([P, E * P + E], F32, name="d")
-        nc.vector.reciprocal(d[:], root[:])
+        nc.scalar.activation(d[:], deg[:], ACT.Abs_reciprocal_sqrt)
 
         part0 = held.tile([P, P], F32, name="part0")
         part1 = held.tile([P, P], F32, name="part1")

@@ -19,16 +19,16 @@ def tile_densegcn_kernel(tc, base, x, w, adjT, b, offs, out):
         adj = held.tile([P, E * P], BF16, name="adj")
         nc.sync.dma_start(adj[:, 0:P], adjT[0])
         nc.scalar.dma_start(adj[:, P : 2 * P], adjT[1])
-        offsets = held.tile([P, P // 16], U16, name="offsets")
-        nc.sync.dma_start(offsets[:], offs)
         x_sb = held.tile([P, P], BF16, name="x_sb")
         nc.sync.dma_start(x_sb[:], x)
         w_sb = held.tile([P, P], BF16, name="w_sb")
         nc.scalar.dma_start(w_sb[:], w)
-        window = held.tile([P, SLOTS], F32, name="window")
-        nc.gpsimd.dma_start(window[:], base)
         bias = held.tile([P, 1], F32, name="bias")
-        nc.gpsimd.dma_start(bias[:], b)
+        nc.scalar.dma_start(bias[:], b)
+        offsets = held.tile([P, P // 16], U16, name="offsets")
+        nc.sync.dma_start(offsets[:], offs)
+        window = held.tile([P, SLOTS], F32, name="window")
+        nc.sync.dma_start(window[:], base)
 
         ones = held.tile([P, P], BF16, name="ones")
         nc.vector.memset(ones[:], 1.0)

@@ -33,14 +33,15 @@ def tile_densegcn_kernel(tc, base, x, w, adjT, b, offs, out):
         ones = held.tile([P, P], BF16, name="ones")
         nc.vector.memset(ones[:], 1.0)
 
-        deg = psum.tile([P, E * P + E], F32, name="deg")
-        nc.tensor.matmul(deg[:, 0 : E * P], ones[:], adj[:], start=True, stop=True)
+        deg_row = psum.tile([P, E * P], F32, name="deg_row")
+        nc.tensor.matmul(deg_row[:], ones[:], adj[:], start=True, stop=True)
+        deg_col = psum.tile([P, E], F32, name="deg_col")
         for e in range(E):
-            nc.tensor.matmul(
-                deg[:, E * P + e : E * P + e + 1], adj[:, e * P : (e + 1) * P], ones[:, 0:1], start=True, stop=True
-            )
-        d = held.tile([P, E * P + E], F32, name="d")
-        nc.scalar.activation(d[:], deg[:], ACT.Abs_reciprocal_sqrt)
+            nc.tensor.matmul(deg_col[:, e : e + 1], adj[:, e * P : (e + 1) * P], ones[:, 0:1], start=True, stop=True)
+        d_row = held.tile([P, E * P], F32, name="d_row")
+        nc.scalar.activation(d_row[:], deg_row[:], ACT.Abs_reciprocal_sqrt)
+        d_col = held.tile([P, E], F32, name="d_col")
+        nc.scalar.activation(d_col[:], deg_col[:], ACT.Abs_reciprocal_sqrt)
 
         part0 = held.tile([P, P], F32, name="part0")
         part1 = held.tile([P, P], F32, name="part1")
@@ -48,8 +49,8 @@ def tile_densegcn_kernel(tc, base, x, w, adjT, b, offs, out):
             nc.vector.scalar_tensor_tensor(
                 part[:],
                 adj[:, e * P : (e + 1) * P],
-                d[:, E * P + e : E * P + e + 1],
-                d[:, e * P : (e + 1) * P],
+                d_col[:, e : e + 1],
+                d_row[:, e * P : (e + 1) * P],
                 ALU.mult,
                 ALU.mult,
             )
@@ -61,12 +62,14 @@ def tile_densegcn_kernel(tc, base, x, w, adjT, b, offs, out):
         h = held.tile([P, P], BF16, name="h")
         nc.vector.tensor_copy(h[:], h_ps[:])
 
-        v_ps = psum.tile([P, P], F32, name="v_ps")
-        nc.tensor.matmul(v_ps[:], h[:], an[:], start=True, stop=True)
+        v_ps_scalar = psum.tile([P, P], F32, name="v_ps_scalar")
+        v_ps_vector = psum.tile([P, P], F32, name="v_ps_vector")
+        nc.tensor.matmul(v_ps_scalar[:], h[:], an[:], start=True, stop=True)
+        nc.tensor.matmul(v_ps_vector[:], h[:], an[:], start=True, stop=True)
         sig = held.tile([P, P], F32, name="sig")
-        nc.scalar.activation(sig[:], v_ps[:], ACT.Sigmoid, bias=bias[:])
+        nc.scalar.activation(sig[:], v_ps_scalar[:], ACT.Sigmoid, bias=bias[:])
         v = held.tile([P, P], F32, name="v")
-        nc.vector.tensor_scalar(v[:], v_ps[:], bias[:], None, ALU.add)
+        nc.vector.tensor_scalar(v[:], v_ps_vector[:], bias[:], None, ALU.add)
 
         nc.vector.tensor_tensor(window[:].indirect(offsets[:]), v[:], sig[:], ALU.mult)
         nc.sync.dma_start(out, window[:])

@@ -22,9 +22,9 @@ def tile_densegcn_kernel(tc, base, x, w, adjT, b, offs, out):
         x_sb = held.tile([P, P], BF16, name="x_sb")
         nc.sync.dma_start(x_sb[:], x)
         w_sb = held.tile([P, P], BF16, name="w_sb")
-        nc.scalar.dma_start(w_sb[:], w)
+        nc.sync.dma_start(w_sb[:], w)
         bias = held.tile([P, 1], F32, name="bias")
-        nc.scalar.dma_start(bias[:], b)
+        nc.sync.dma_start(bias[:], b)
         offsets = held.tile([P, P // 16], U16, name="offsets")
         nc.sync.dma_start(offsets[:], offs)
         window = held.tile([P, SLOTS], F32, name="window")

@@ -17,18 +17,17 @@ def tile_densegcn_kernel(tc, base, x, w, adjT, b, offs, out):
     nc = tc.nc
     with tc.tile_pool(name="held", bufs=1) as held, tc.psum_pool(name="psum", bufs=1) as psum:
         adj = held.tile([P, E * P], BF16, name="adj")
-        nc.sync.dma_start(adj[:, 0:P], adjT[0])
-        nc.scalar.dma_start(adj[:, P : 2 * P], adjT[1])
+        nc.sync.dma_start(adj[:].rearrange("u (e j) -> u e j", e=E), adjT.rearrange("e u j -> u e j"))
         x_sb = held.tile([P, P], BF16, name="x_sb")
-        nc.sync.dma_start(x_sb[:], x)
+        nc.scalar.dma_start(x_sb[:], x)
         w_sb = held.tile([P, P], BF16, name="w_sb")
-        nc.sync.dma_start(w_sb[:], w)
+        nc.scalar.dma_start(w_sb[:], w)
         bias = held.tile([P, 1], F32, name="bias")
         nc.sync.dma_start(bias[:], b)
         offsets = held.tile([P, P // 16], U16, name="offsets")
         nc.sync.dma_start(offsets[:], offs)
         window = held.tile([P, SLOTS], F32, name="window")
-        nc.sync.dma_start(window[:], base)
+        nc.scalar.dma_start(window[:], base)
 
         ones = held.tile([P, P], BF16, name="ones")
         nc.vector.memset(ones[:], 1.0)

@@ -42,19 +42,12 @@ def tile_densegcn_kernel(tc, base, x, w, adjT, b, offs, out):
         d_col = held.tile([P, E], F32, name="d_col")
         nc.scalar.activation(d_col[:], deg_col[:], ACT.Abs_reciprocal_sqrt)
 
+        scaled1 = held.tile([P, P], F32, name="scaled1")
+        nc.vector.tensor_tensor(scaled1[:], adj[:, P : 2 * P], d_row[:, P : 2 * P], ALU.mult)
         part0 = held.tile([P, P], F32, name="part0")
-        part1 = held.tile([P, P], F32, name="part1")
-        for e, part in enumerate((part0, part1)):
-            nc.vector.scalar_tensor_tensor(
-                part[:],
-                adj[:, e * P : (e + 1) * P],
-                d_col[:, e : e + 1],
-                d_row[:, e * P : (e + 1) * P],
-                ALU.mult,
-                ALU.mult,
-            )
+        nc.vector.scalar_tensor_tensor(part0[:], adj[:, 0:P], d_col[:, 0:1], d_row[:, 0:P], ALU.mult, ALU.mult)
         an = held.tile([P, P], BF16, name="an")
-        nc.vector.tensor_tensor(an[:], part0[:], part1[:], ALU.add)
+        nc.vector.scalar_tensor_tensor(an[:], scaled1[:], d_col[:, 1:2], part0[:], ALU.mult, ALU.add)
 
         h_ps = psum.tile([P, P], F32, name="h_ps")
         nc.tensor.matmul(h_ps[:], x_sb[:], w_sb[:], start=True, stop=True)

@@ -32,7 +32,7 @@ def tile_densegcn_kernel(tc, base, x, w, adjT, b, offs, out):
         ones = held.tile([P, P], BF16, name="ones")
         nc.vector.memset(ones[:], 1.0)
 
-        deg_row = psum.tile([P, E * P], F32, name="deg_row")
+        deg_row = psum.tile([P, E * P], F32, name="deg_row", tag="deg_row_then_h")
         nc.tensor.matmul(deg_row[:], ones[:], adj[:], start=True, stop=True)
         deg_col = psum.tile([P, E], F32, name="deg_col")
         for e in range(E):
@@ -49,7 +49,7 @@ def tile_densegcn_kernel(tc, base, x, w, adjT, b, offs, out):
         an = held.tile([P, P], BF16, name="an")
         nc.vector.scalar_tensor_tensor(an[:], scaled1[:], d_col[:, 1:2], part0[:], ALU.mult, ALU.add)
 
-        h_ps = psum.tile([P, P], F32, name="h_ps")
+        h_ps = psum.tile([P, P], F32, name="h_ps", tag="deg_row_then_h")
         nc.tensor.matmul(h_ps[:], x_sb[:], w_sb[:], start=True, stop=True)
         h = held.tile([P, P], BF16, name="h")
         nc.vector.tensor_copy(h[:], h_ps[:])

@@ -56,8 +56,8 @@ def tile_densegcn_kernel(tc, base, x, w, adjT, b, offs, out):
 
         v_ps_scalar = psum.tile([P, P], F32, name="v_ps_scalar")
         v_ps_vector = psum.tile([P, P], F32, name="v_ps_vector")
-        nc.tensor.matmul(v_ps_scalar[:], h[:], an[:], start=True, stop=True)
         nc.tensor.matmul(v_ps_vector[:], h[:], an[:], start=True, stop=True)
+        nc.tensor.matmul(v_ps_scalar[:], h[:], an[:], start=True, stop=True)
         sig = held.tile([P, P], F32, name="sig")
         nc.scalar.activation(sig[:], v_ps_scalar[:], ACT.Sigmoid, bias=bias[:])
         v = held.tile([P, P], F32, name="v")

@@ -32,13 +32,16 @@ def tile_densegcn_kernel(tc, base, x, w, adjT, b, offs, out):
         ones = held.tile([P, P], BF16, name="ones")
         nc.vector.memset(ones[:], 1.0)
 
-        deg_row = psum.tile([P, E * P], F32, name="deg_row", tag="deg_row_then_h")
-        nc.tensor.matmul(deg_row[:], ones[:], adj[:], start=True, stop=True)
+        deg_row0 = psum.tile([P, P], F32, name="deg_row0")
+        deg_row1 = psum.tile([P, P], F32, name="deg_row1", tag="deg_row1_then_h")
+        for e, deg_row in enumerate((deg_row0, deg_row1)):
+            nc.tensor.matmul(deg_row[:], ones[:], adj[:, e * P : (e + 1) * P], start=True, stop=True)
         deg_col = psum.tile([P, E], F32, name="deg_col")
         for e in range(E):
             nc.tensor.matmul(deg_col[:, e : e + 1], adj[:, e * P : (e + 1) * P], ones[:, 0:1], start=True, stop=True)
         d_row = held.tile([P, E * P], F32, name="d_row")
-        nc.scalar.activation(d_row[:], deg_row[:], ACT.Abs_reciprocal_sqrt)
+        for e, deg_row in enumerate((deg_row0, deg_row1)):
+            nc.scalar.activation(d_row[:, e * P : (e + 1) * P], deg_row[:], ACT.Abs_reciprocal_sqrt)
         d_col = held.tile([P, E], F32, name="d_col")
         nc.scalar.activation(d_col[:], deg_col[:], ACT.Abs_reciprocal_sqrt)
 
@@ -49,7 +52,7 @@ def tile_densegcn_kernel(tc, base, x, w, adjT, b, offs, out):
         an = held.tile([P, P], BF16, name="an")
         nc.vector.scalar_tensor_tensor(an[:], scaled1[:], d_col[:, 1:2], part0[:], ALU.mult, ALU.add)
 
-        h_ps = psum.tile([P, P], F32, name="h_ps", tag="deg_row_then_h")
+        h_ps = psum.tile([P, P], F32, name="h_ps", tag="deg_row1_then_h")
         nc.tensor.matmul(h_ps[:], x_sb[:], w_sb[:], start=True, stop=True)
         h = held.tile([P, P], BF16, name="h")
         nc.vector.tensor_copy(h[:], h_ps[:])

@@ -50,7 +50,9 @@ def tile_densegcn_kernel(tc, base, x, w, adjT, b, offs, out):
         part0 = held.tile([P, P], F32, name="part0")
         nc.vector.scalar_tensor_tensor(part0[:], adj[:, 0:P], d_col[:, 0:1], d_row[:, 0:P], ALU.mult, ALU.mult)
         an = held.tile([P, P], BF16, name="an")
-        nc.vector.scalar_tensor_tensor(an[:], scaled1[:], d_col[:, 1:2], part0[:], ALU.mult, ALU.add)
+        halves = (slice(0, P // 2), slice(P // 2, P))
+        for half in halves:
+            nc.vector.scalar_tensor_tensor(an[:, half], scaled1[:, half], d_col[:, 1:2], part0[:, half], ALU.mult, ALU.add)
 
         h_ps = psum.tile([P, P], F32, name="h_ps", tag="deg_row1_then_h")
         nc.tensor.matmul(h_ps[:], x_sb[:], w_sb[:], start=True, stop=True)
@@ -58,13 +60,14 @@ def tile_densegcn_kernel(tc, base, x, w, adjT, b, offs, out):
         nc.vector.tensor_copy(h[:], h_ps[:])
 
         v_ps_scalar = psum.tile([P, P], F32, name="v_ps_scalar")
-        v_ps_vector = psum.tile([P, P], F32, name="v_ps_vector")
-        nc.tensor.matmul(v_ps_vector[:], h[:], an[:], start=True, stop=True)
+        v = held.tile([P, P], F32, name="v")
+        for i, half in enumerate(halves):
+            v_ps_half = psum.tile([P, P // 2], F32, name=f"v_ps_half{i}")
+            nc.tensor.matmul(v_ps_half[:], h[:], an[:, half], start=True, stop=True)
+            nc.vector.tensor_scalar(v[:, half], v_ps_half[:], bias[:], None, ALU.add)
         nc.tensor.matmul(v_ps_scalar[:], h[:], an[:], start=True, stop=True)
         sig = held.tile([P, P], F32, name="sig")
         nc.scalar.activation(sig[:], v_ps_scalar[:], ACT.Sigmoid, bias=bias[:])
-        v = held.tile([P, P], F32, name="v")
-        nc.vector.tensor_scalar(v[:], v_ps_vector[:], bias[:], None, ALU.add)
 
         nc.vector.tensor_tensor(window[:].indirect(offsets[:]), v[:], sig[:], ALU.mult)
         nc.sync.dma_start(out, window[:])

@@ -1,4 +1,5 @@
 import concourse.mybir as mybir
+from concourse.masks import make_identity
 
 F32 = mybir.dt.float32
 BF16 = mybir.dt.bfloat16
@@ -29,35 +30,39 @@ def tile_densegcn_kernel(tc, base, x, w, adjT, b, offs, out):
         window = held.tile([P, SLOTS], F32, name="window")
         nc.scalar.dma_start(window[:], base)
 
+        identity = held.tile([P, P], F32, name="identity")
+        make_identity(nc, identity[:])
         ones = held.tile([P, P], BF16, name="ones")
-        nc.vector.memset(ones[:], 1.0)
+        nc.gpsimd.memset(ones[:], 1.0)
 
-        deg_row0 = psum.tile([P, P], F32, name="deg_row0")
-        deg_row1 = psum.tile([P, P], F32, name="deg_row1", tag="deg_row1_then_h")
-        for e, deg_row in enumerate((deg_row0, deg_row1)):
-            nc.tensor.matmul(deg_row[:], ones[:], adj[:, e * P : (e + 1) * P], start=True, stop=True)
-        deg_col = psum.tile([P, E], F32, name="deg_col")
+        deg_col = psum.tile([P, E], F32, name="deg_col", tag="deg_col_then_h")
         for e in range(E):
             nc.tensor.matmul(deg_col[:, e : e + 1], adj[:, e * P : (e + 1) * P], ones[:, 0:1], start=True, stop=True)
-        d_row = held.tile([P, E * P], F32, name="d_row")
-        for e, deg_row in enumerate((deg_row0, deg_row1)):
-            nc.scalar.activation(d_row[:, e * P : (e + 1) * P], deg_row[:], ACT.Abs_reciprocal_sqrt)
         d_col = held.tile([P, E], F32, name="d_col")
         nc.scalar.activation(d_col[:], deg_col[:], ACT.Abs_reciprocal_sqrt)
+        deg_row0 = psum.tile([P, P], F32, name="deg_row0")
+        nc.tensor.matmul(deg_row0[:], ones[:], adj[:, 0:P], start=True, stop=True)
+        d_row0 = held.tile([P, P], F32, name="d_row0")
+        nc.scalar.activation(d_row0[:], deg_row0[:], ACT.Abs_reciprocal_sqrt)
 
-        scaled1 = held.tile([P, P], F32, name="scaled1")
-        nc.vector.tensor_tensor(scaled1[:], adj[:, P : 2 * P], d_row[:, P : 2 * P], ALU.mult)
-        part0 = held.tile([P, P], F32, name="part0")
-        nc.vector.scalar_tensor_tensor(part0[:], adj[:, 0:P], d_col[:, 0:1], d_row[:, 0:P], ALU.mult, ALU.mult)
-        an = held.tile([P, P], BF16, name="an")
-        halves = (slice(0, P // 2), slice(P // 2, P))
-        for half in halves:
-            nc.vector.scalar_tensor_tensor(an[:, half], scaled1[:, half], d_col[:, 1:2], part0[:, half], ALU.mult, ALU.add)
-
-        h_ps = psum.tile([P, P], F32, name="h_ps", tag="deg_row1_then_h")
+        h_ps = psum.tile([P, P], F32, name="h_ps", tag="deg_col_then_h")
         nc.tensor.matmul(h_ps[:], x_sb[:], w_sb[:], start=True, stop=True)
         h = held.tile([P, P], BF16, name="h")
         nc.vector.tensor_copy(h[:], h_ps[:])
+
+        d_row1 = psum.tile([P, P], F32, name="d_row1")
+        nc.tensor.transpose(d_row1[:], d_col[:, 1:2].to_broadcast([P, P]), identity[:])
+        scaled1 = held.tile([P, P], F32, name="scaled1")
+        nc.vector.tensor_scalar(scaled1[:], adj[:, P : 2 * P], d_col[:, 1:2], None, ALU.mult)
+        part0 = held.tile([P, P], F32, name="part0")
+        nc.vector.scalar_tensor_tensor(part0[:], adj[:, 0:P], d_col[:, 0:1], d_row0[:], ALU.mult, ALU.mult)
+        halves = (slice(0, P // 2), slice(P // 2, P))
+        part1 = held.tile([P, P], F32, name="part1")
+        an = held.tile([P, P], BF16, name="an")
+        for half in halves:
+            nc.vector.tensor_tensor(part1[:, half], scaled1[:, half], d_row1[:, half], ALU.mult)
+        for half in halves:
+            nc.vector.tensor_tensor(an[:, half], part1[:, half], part0[:, half], ALU.add)
 
         v_ps_scalar = psum.tile([P, P], F32, name="v_ps_scalar")
         v = held.tile([P, P], F32, name="v")

import concourse.mybir as mybir
from concourse.masks import make_identity

F32 = mybir.dt.float32
BF16 = mybir.dt.bfloat16
U16 = mybir.dt.uint16
ACT = mybir.ActivationFunctionType
ALU = mybir.AluOpType

P = 128
E = 2
SLOTS = 256

FLOPS = 2 * P * P * P * 2


def tile_densegcn_kernel(tc, base, x, w, adjT, b, offs, out):
    nc = tc.nc
    with tc.tile_pool(name="held", bufs=1) as held, tc.psum_pool(name="psum", bufs=1) as psum:
        adj = held.tile([P, E * P], BF16, name="adj")
        nc.sync.dma_start(adj[:].rearrange("u (e j) -> u e j", e=E), adjT.rearrange("e u j -> u e j"))
        x_sb = held.tile([P, P], BF16, name="x_sb")
        nc.scalar.dma_start(x_sb[:], x)
        w_sb = held.tile([P, P], BF16, name="w_sb")
        nc.scalar.dma_start(w_sb[:], w)
        bias = held.tile([P, 1], F32, name="bias")
        nc.sync.dma_start(bias[:], b)
        offsets = held.tile([P, P // 16], U16, name="offsets")
        nc.sync.dma_start(offsets[:], offs)
        window = held.tile([P, SLOTS], F32, name="window")
        nc.scalar.dma_start(window[:], base)

        identity = held.tile([P, P], F32, name="identity")
        make_identity(nc, identity[:])
        ones = held.tile([P, P], BF16, name="ones")
        nc.gpsimd.memset(ones[:], 1.0)

        deg_col = psum.tile([P, E], F32, name="deg_col", tag="deg_col_then_h")
        for e in range(E):
            nc.tensor.matmul(deg_col[:, e : e + 1], adj[:, e * P : (e + 1) * P], ones[:, 0:1], start=True, stop=True)
        d_col = held.tile([P, E], F32, name="d_col")
        nc.scalar.activation(d_col[:], deg_col[:], ACT.Abs_reciprocal_sqrt)
        deg_row0 = psum.tile([P, P], F32, name="deg_row0")
        nc.tensor.matmul(deg_row0[:], ones[:], adj[:, 0:P], start=True, stop=True)
        d_row0 = held.tile([P, P], F32, name="d_row0")
        nc.scalar.activation(d_row0[:], deg_row0[:], ACT.Abs_reciprocal_sqrt)

        h_ps = psum.tile([P, P], F32, name="h_ps", tag="deg_col_then_h")
        nc.tensor.matmul(h_ps[:], x_sb[:], w_sb[:], start=True, stop=True)
        h = held.tile([P, P], BF16, name="h")
        nc.vector.tensor_copy(h[:], h_ps[:])

        d_row1 = psum.tile([P, P], F32, name="d_row1")
        nc.tensor.transpose(d_row1[:], d_col[:, 1:2].to_broadcast([P, P]), identity[:])
        scaled1 = held.tile([P, P], F32, name="scaled1")
        nc.vector.tensor_scalar(scaled1[:], adj[:, P : 2 * P], d_col[:, 1:2], None, ALU.mult)
        part0 = held.tile([P, P], F32, name="part0")
        nc.vector.scalar_tensor_tensor(part0[:], adj[:, 0:P], d_col[:, 0:1], d_row0[:], ALU.mult, ALU.mult)
        halves = (slice(0, P // 2), slice(P // 2, P))
        part1 = held.tile([P, P], F32, name="part1")
        an = held.tile([P, P], BF16, name="an")
        for half in halves:
            nc.vector.tensor_tensor(part1[:, half], scaled1[:, half], d_row1[:, half], ALU.mult)
        for half in halves:
            nc.vector.tensor_tensor(an[:, half], part1[:, half], part0[:, half], ALU.add)

        v_ps_scalar = psum.tile([P, P], F32, name="v_ps_scalar")
        v = held.tile([P, P], F32, name="v")
        for i, half in enumerate(halves):
            v_ps_half = psum.tile([P, P // 2], F32, name=f"v_ps_half{i}")
            nc.tensor.matmul(v_ps_half[:], h[:], an[:, half], start=True, stop=True)
            nc.vector.tensor_scalar(v[:, half], v_ps_half[:], bias[:], None, ALU.add)
        nc.tensor.matmul(v_ps_scalar[:], h[:], an[:], start=True, stop=True)
        sig = held.tile([P, P], F32, name="sig")
        nc.scalar.activation(sig[:], v_ps_scalar[:], ACT.Sigmoid, bias=bias[:])

        nc.vector.tensor_tensor(window[:].indirect(offsets[:]), v[:], sig[:], ALU.mult)
        nc.sync.dma_start(out, window[:])
